import numpy as np
import ml_dtypes


def mxq(x, axis, fmt="e4m3"):
    dtype, down = {"e4m3": (ml_dtypes.float8_e4m3fn, 7), "e5m2": (ml_dtypes.float8_e5m2, 14)}[fmt]
    v = np.moveaxis(np.asarray(x, np.float32).astype(ml_dtypes.bfloat16).astype(np.float64), axis, -1)
    blocks = v.reshape(v.shape[:-1] + (-1, 32))
    amax = np.abs(blocks).max(-1, keepdims=True)
    byte = np.maximum(np.where(amax > 0, np.frexp(amax)[1] - 1 + 127, 0) - down, 1)
    scale = np.exp2(byte - 127.0)
    codes = (blocks / scale).astype(np.float32).astype(dtype).astype(np.float64)
    return np.moveaxis((codes * scale).reshape(v.shape), -1, axis)


WIDE = False


def mx_kscale(k):
    if not WIDE:
        return np.ones(k)
    levels = np.array([10, -10, 5, -5, 0])
    a = np.random.permutation(np.resize(levels, k // 512 * 4)).reshape(k // 512, 4)
    idx = np.arange(k)
    return np.exp2(a[idx // 512, idx % 128 // 32])


BF16 = ml_dtypes.bfloat16


def bf(x):
    return np.asarray(x, np.float32).astype(BF16)


def f64(x):
    return np.asarray(x).astype(np.float64)


E2M1 = np.array([0.0, 0.5, 1.0, 1.5, 2.0, 3.0, 4.0, 6.0, -0.0, -0.5, -1.0, -1.5, -2.0, -3.0, -4.0, -6.0])


def pack_weight(w, fmt):
    k, n = w.shape
    w = f64(bf(w)).reshape(k // 32, 32, n)
    amax = np.abs(w).max(1)
    if fmt == "e4m3":
        byte = np.frexp(amax)[1] - 1 + 127 - 7
    else:
        mant, ex = np.frexp(amax / 6.0)
        byte = np.where(mant > 0.5, ex, ex - 1) + 127
    byte = np.clip(np.where(amax > 0, byte, 1), 1, 254)
    scaled = (w * np.exp2(127.0 - byte)[:, None, :]).reshape(k, n).astype(np.float32)
    by_word = np.ascontiguousarray(scaled.reshape(k // 512, 128, 4, n).transpose(0, 1, 3, 2))
    if fmt == "e4m3":
        words = by_word.astype(ml_dtypes.float8_e4m3fn).view(np.uint8)
    else:
        c = by_word.astype(ml_dtypes.float4_e2m1fn).view(np.uint8) & 0xF
        words = c[..., 0::2] | (c[..., 1::2] << 4)
    return np.ascontiguousarray(words), np.ascontiguousarray(byte.astype(np.uint8).reshape(k // 512, 16, n))


def unpack_weight(words, scales, fmt):
    g, p, n, _ = words.shape
    if fmt == "e4m3":
        vals = np.ascontiguousarray(words).view(ml_dtypes.float8_e4m3fn).astype(np.float64)
    else:
        nib = np.empty((g, p, n, 4), np.uint8)
        nib[..., 0::2] = words & 0xF
        nib[..., 1::2] = words >> 4
        vals = E2M1[nib]
    vals = vals * np.repeat(np.exp2(scales.astype(np.float64) - 127.0), 8, axis=1)[..., None]
    return vals.transpose(0, 1, 3, 2).reshape(g * 512, n)


B, D_IN, HID, OUT = 512, 1024, 4096, 1024


def setup_inputs():
    s, t = mx_kscale(D_IN), mx_kscale(HID)
    u = np.concatenate([s, t])
    x = bf(np.random.standard_normal((B, D_IN)) * s)
    W1 = np.random.standard_normal((HID, D_IN)) / np.sqrt(D_IN) / s[None, :] * t[:, None]
    W1_words, W1_scales = pack_weight(np.ascontiguousarray(W1.T), "e4m3")
    b1 = bf(np.random.standard_normal(HID) * 0.3 * t)
    W2 = np.random.standard_normal((OUT, D_IN + HID)) / np.sqrt(D_IN + HID) / u[None, :]
    W2_words, W2_scales = pack_weight(np.ascontiguousarray(W2.T), "e4m3")
    b2 = bf(np.random.standard_normal(OUT) * 0.3)
    return {"x": x,
            "W1_words": W1_words,
            "W1_scales": W1_scales,
            "b1": b1,
            "W2_words": W2_words,
            "W2_scales": W2_scales,
            "b2": b2}


def reference(x, W1_words, W1_scales, b1, W2_words, W2_scales, b2):
    xq = mxq(f64(x), 1, "e4m3")
    h1 = np.maximum((xq @ unpack_weight(W1_words, W1_scales, "e4m3")) + f64(b1), 0.0)
    concat = np.concatenate([xq, mxq(h1, 1, "e4m3")], axis=1)
    return (concat @ unpack_weight(W2_words, W2_scales, "e4m3")) + f64(b2)

@@ -1,0 +1,224 @@
+from contextlib import ExitStack
+
+import concourse.mybir as mybir
+from concourse.masks import make_identity
+
+BF16 = mybir.dt.bfloat16
+F32 = mybir.dt.float32
+I32 = mybir.dt.int32
+U32 = mybir.dt.uint32
+U8 = mybir.dt.uint8
+FP8X4 = mybir.dt.float8_e4m3fn_x4
+ADD = mybir.AluOpType.add
+RELU = mybir.ActivationFunctionType.Relu
+
+BATCH, D_IN, HID, D_OUT = 512, 1024, 4096, 1024
+FLOPS = 2 * BATCH * D_IN * HID + 2 * BATCH * (D_IN + HID) * D_OUT
+
+P = 128
+PACK = 4
+K_PASS = P * PACK
+N_PASS = 512
+ROW_TILES = BATCH // P
+X_GROUPS = D_IN // K_PASS
+H_GROUPS = HID // K_PASS
+C_GROUPS = X_GROUPS + H_GROUPS
+OUT_HALVES = D_OUT // N_PASS
+SCALE_ROWS = 4
+PLANES = 4
+QUADRANTS = 4
+W2_SLOTS = (C_GROUPS + PLANES - 1) // PLANES
+
+
+def piece(i, width):
+    return slice(i * width, (i + 1) * width)
+
+
+def tile_dpn_kernel(tc, x, W1_words, W1_scales, b1, W2_words, W2_scales, b2, out):
+    nc = tc.nc
+    with ExitStack() as stack:
+        stack.enter_context(tc.manual_schedule())
+        keep = stack.enter_context(tc.tile_pool(name="keep", bufs=1))
+        x_stage = stack.enter_context(tc.tile_pool(name="x_stage", bufs=2))
+        h_stage = stack.enter_context(tc.tile_pool(name="h_stage", bufs=2 * ROW_TILES))
+        q_stage = stack.enter_context(tc.tile_pool(name="q_stage", bufs=3))
+        o_stage = stack.enter_context(tc.tile_pool(name="o_stage", bufs=4))
+        sums_psum = stack.enter_context(tc.psum_pool(name="sums_psum", bufs=4))
+        turn_psum = stack.enter_context(tc.psum_pool(name="turn_psum", bufs=4))
+
+        x_sb = keep.tile([P, ROW_TILES, D_IN], BF16)
+        w1_words = keep.tile([P, X_GROUPS, HID], U32, align_bytes=64)
+        w1_planes = keep.tile([P, HID], U8, align_bytes=64)
+        w2_words = keep.tile([P, C_GROUPS, D_OUT], U32, align_bytes=64)
+        w2_planes = keep.tile([P, W2_SLOTS, D_OUT], U8, align_bytes=64)
+        b1_all = keep.tile([P, HID], BF16)
+        b2_all = keep.tile([P, D_OUT], BF16)
+        c_codes = keep.tile([P, C_GROUPS, BATCH], U32, align_bytes=64)
+        c_planes = keep.tile([P, C_GROUPS, BATCH], U8, align_bytes=64)
+        ident_f32 = keep.tile([P, P], F32)
+        ident_bf16 = keep.tile([P, P], BF16)
+
+        nc.vector.memset(w1_planes[:].bitcast(I32), 0)
+        nc.vector.memset(w2_planes[:].bitcast(I32), 0)
+        make_identity(nc, ident_f32[:])
+        make_identity(nc, ident_bf16[:])
+
+        for r in range(ROW_TILES):
+            nc.sync.dma_start(out=x_sb[:, r, :], in_=x[piece(r, P), :])
+        w1_by_partition = W1_words.rearrange("g p n t -> p g (n t)")
+
+        def load_w1_piece(j):
+            nc.sync.dma_start(
+                out=w1_words[:, :, piece(j, N_PASS)].bitcast(I32),
+                in_=w1_by_partition[:, :, piece(j, N_PASS * PACK)].bitcast(I32),
+            )
+            nc.sync.dma_start(
+                out=b1_all[:, piece(j, N_PASS)], in_=b1[piece(j, N_PASS)].partition_broadcast(P)
+            )
+
+        def load_w1_planes():
+            for quad in range(QUADRANTS):
+                first = 32 * quad
+                nc.sync.dma_start(
+                    out=w1_planes[first : first + SCALE_ROWS * X_GROUPS, :].bitcast(I32),
+                    in_=W1_scales[:, piece(quad, SCALE_ROWS), :].bitcast(I32),
+                )
+
+        load_w1_planes()
+        for j in range(H_GROUPS):
+            load_w1_piece(j)
+        for slot in range(W2_SLOTS):
+            groups = min(PLANES, C_GROUPS - slot * PLANES)
+            for quad in range(QUADRANTS):
+                first = 32 * quad
+                nc.sync.dma_start(
+                    out=w2_planes[first : first + SCALE_ROWS * groups, slot, :].bitcast(I32),
+                    in_=W2_scales[
+                        slot * PLANES : slot * PLANES + groups, piece(quad, SCALE_ROWS), :
+                    ].bitcast(I32),
+                )
+        for g in range(C_GROUPS):
+            nc.sync.dma_start(
+                out=w2_words[:, g, :].bitcast(I32),
+                in_=W2_words[g].rearrange("p n t -> p (n t)").bitcast(I32),
+            )
+        nc.sync.dma_start(out=b2_all[:], in_=b2.partition_broadcast(P))
+
+        x_pairs = x_sb[:].bitcast(F32)
+        pairs_per_pass = K_PASS // 2
+        for r in range(ROW_TILES):
+            x_turned = turn_psum.tile([P, X_GROUPS, 2, P], F32, tag="turn")
+            for g in range(X_GROUPS):
+                for u in range(2):
+                    nc.tensor.transpose(
+                        x_turned[:, g, u, :],
+                        x_pairs[:, r, g * pairs_per_pass + u : (g + 1) * pairs_per_pass : 2],
+                        ident_f32[:],
+                    )
+            x_grouped = x_stage.tile([P, X_GROUPS, P * PACK], BF16, align_bytes=64)
+            nc.scalar.copy(
+                out=x_grouped[:].bitcast(F32).rearrange("p g (b u) -> p g b u", u=2),
+                in_=x_turned[:].rearrange("p g u b -> p g b u"),
+            )
+            for g in range(X_GROUPS):
+                nc.vector.quantize_mx(
+                    out=c_codes[:, g, piece(r, P)].bitcast(FP8X4),
+                    scales=c_planes[:, g, piece(r, P)],
+                    in_=x_grouped[:, g, :],
+                )
+
+        def first_product(j):
+            pre_relu = []
+            for r in range(ROW_TILES):
+                sums = sums_psum.tile([P, N_PASS], F32, tag="sums")
+                for g in range(X_GROUPS):
+                    nc.tensor.matmul_mx(
+                        out=sums[:],
+                        lhsT=c_codes[:, g, piece(r, P)].bitcast(FP8X4),
+                        lhsT_scale=c_planes[:, g, piece(r, P)],
+                        rhs=w1_words[:, g, piece(j, N_PASS)].bitcast(FP8X4),
+                        rhs_scale=w1_planes[SCALE_ROWS * g : P, piece(j, N_PASS)],
+                        start=(g == 0),
+                        stop=(g == X_GROUPS - 1),
+                    )
+                sorted_rows = h_stage.tile([P, PACK, P], BF16, tag="sorted_rows")
+                nc.vector.tensor_tensor(
+                    out=sorted_rows[:],
+                    in0=sums[:].rearrange("p (q t) -> p t q", t=PACK),
+                    in1=b1_all[:, piece(j, N_PASS)].rearrange("p (q t) -> p t q", t=PACK),
+                    op=ADD,
+                )
+                pre_relu.append(sorted_rows)
+            return pre_relu
+
+        def turn_and_relu(pre_relu):
+            grouped = q_stage.tile([P, BATCH, PACK], BF16, tag="grouped", align_bytes=64)
+            rows_per_bank = 2 * P
+            for pair in range(ROW_TILES // 2):
+                turned = turn_psum.tile([P, PACK, rows_per_bank], BF16, tag="turn")
+                for i in range(2):
+                    for t in range(PACK):
+                        nc.tensor.transpose(
+                            turned[:, t, piece(i, P)], pre_relu[2 * pair + i][:, t, :], ident_bf16[:]
+                        )
+                nc.scalar.activation(
+                    out=grouped[:, piece(pair, rows_per_bank), :],
+                    in_=turned[:].rearrange("p t b -> p b t"),
+                    func=RELU,
+                )
+            return grouped
+
+        def quantise_h(j, grouped):
+            nc.vector.quantize_mx(
+                out=c_codes[:, X_GROUPS + j, :].bitcast(FP8X4),
+                scales=c_planes[:, X_GROUPS + j, :],
+                in_=grouped[:].rearrange("p b t -> p (b t)"),
+            )
+
+        def second_product_pass(acc, r, half, g):
+            nc.tensor.matmul_mx(
+                out=acc[:],
+                lhsT=c_codes[:, g, piece(r, P)].bitcast(FP8X4),
+                lhsT_scale=c_planes[:, g, piece(r, P)],
+                rhs=w2_words[:, g, piece(half, N_PASS)].bitcast(FP8X4),
+                rhs_scale=w2_planes[SCALE_ROWS * (g % PLANES) : P, g // PLANES, piece(half, N_PASS)],
+                start=(g == 0),
+                stop=(g == C_GROUPS - 1),
+            )
+
+        def finish(acc, r, half):
+            result = o_stage.tile([P, N_PASS], F32, tag="result")
+            nc.vector.tensor_tensor(
+                out=result[:], in0=acc[:], in1=b2_all[:, piece(half, N_PASS)], op=ADD
+            )
+            nc.sync.dma_start(out=out[piece(r, P), piece(half, N_PASS)], in_=result[:])
+
+        pre_relu = {}
+        grouped = {}
+        for j in range(H_GROUPS):
+            pre_relu[j] = first_product(j)
+            if j >= 1:
+                grouped[j - 1] = turn_and_relu(pre_relu[j - 1])
+            if j >= 2:
+                quantise_h(j - 2, grouped[j - 2])
+
+        left = []
+        for r in range(ROW_TILES):
+            acc = sums_psum.tile([P, N_PASS], F32, tag="sums")
+            left.append(acc)
+        for g in range(X_GROUPS):
+            for r in range(ROW_TILES):
+                second_product_pass(left[r], r, 0, g)
+        grouped[H_GROUPS - 1] = turn_and_relu(pre_relu[H_GROUPS - 1])
+        quantise_h(H_GROUPS - 2, grouped[H_GROUPS - 2])
+        quantise_h(H_GROUPS - 1, grouped[H_GROUPS - 1])
+        for g in range(X_GROUPS, C_GROUPS):
+            for r in range(ROW_TILES):
+                second_product_pass(left[r], r, 0, g)
+        for r in range(ROW_TILES):
+            finish(left[r], r, 0)
+        for r in range(ROW_TILES):
+            acc = turn_psum.tile([P, N_PASS], F32, tag="turn")
+            for g in range(C_GROUPS):
+                second_product_pass(acc, r, 1, g)
+            finish(acc, r, 1)

@@ -51,18 +51,21 @@ def tile_dpn_kernel(tc, x, W1_words, W1_scales, b1, W2_words, W2_scales, b2, out
         w1_planes = keep.tile([P, HID], U8, align_bytes=64)
         w2_words = keep.tile([P, C_GROUPS, D_OUT], U32, align_bytes=64)
         w2_planes = keep.tile([P, W2_SLOTS, D_OUT], U8, align_bytes=64)
-        b1_all = keep.tile([P, HID], BF16)
+        bias_rows = keep.tile([P, N_PASS], BF16)
+        b1_sorted = keep.tile([P, H_GROUPS, PACK, P], BF16)
         b2_all = keep.tile([P, D_OUT], BF16)
         c_codes = keep.tile([P, C_GROUPS, BATCH], U32, align_bytes=64)
         c_planes = keep.tile([P, C_GROUPS, BATCH], U8, align_bytes=64)
         ident_f32 = keep.tile([P, P], F32)
         ident_bf16 = keep.tile([P, P], BF16)
 
+        nc.vector.memset(bias_rows[:], 0.0)
         nc.vector.memset(w1_planes[:].bitcast(I32), 0)
         nc.vector.memset(w2_planes[:].bitcast(I32), 0)
         make_identity(nc, ident_f32[:])
         make_identity(nc, ident_bf16[:])
 
+        nc.scalar.dma_start(out=bias_rows[0:H_GROUPS, :], in_=b1.rearrange("(j n) -> j n", n=N_PASS))
         for r in range(ROW_TILES):
             nc.sync.dma_start(out=x_sb[:, r, :], in_=x[piece(r, P), :])
         w1_by_partition = W1_words.rearrange("g p n t -> p g (n t)")
@@ -71,9 +74,6 @@ def tile_dpn_kernel(tc, x, W1_words, W1_scales, b1, W2_words, W2_scales, b2, out
             nc.sync.dma_start(
                 out=w1_words[:, :, piece(j, N_PASS)].bitcast(I32),
                 in_=w1_by_partition[:, :, piece(j, N_PASS * PACK)].bitcast(I32),
-            )
-            nc.sync.dma_start(
-                out=b1_all[:, piece(j, N_PASS)], in_=b1[piece(j, N_PASS)].partition_broadcast(P)
             )
 
         def load_w1_planes():
@@ -103,6 +103,19 @@ def tile_dpn_kernel(tc, x, W1_words, W1_scales, b1, W2_words, W2_scales, b2, out
                 in_=W2_words[g].rearrange("p n t -> p (n t)").bitcast(I32),
             )
         nc.sync.dma_start(out=b2_all[:], in_=b2.partition_broadcast(P))
+
+        def spread_bias(j):
+            spread = turn_psum.tile([P, N_PASS], F32, tag="turn")
+            nc.tensor.matmul(
+                out=spread[:],
+                lhsT=ident_bf16[:, j : j + 1].to_broadcast([P, P]),
+                rhs=bias_rows[:],
+                start=True,
+                stop=True,
+            )
+            nc.scalar.copy(out=b1_sorted[:, j], in_=spread[:].rearrange("p (q t) -> p t q", t=PACK))
+
+        spread_bias(0)
 
         x_pairs = x_sb[:].bitcast(F32)
         pairs_per_pass = K_PASS // 2
@@ -145,7 +158,7 @@ def tile_dpn_kernel(tc, x, W1_words, W1_scales, b1, W2_words, W2_scales, b2, out
                 nc.vector.tensor_tensor(
                     out=sorted_rows[:],
                     in0=sums[:].rearrange("p (q t) -> p t q", t=PACK),
-                    in1=b1_all[:, piece(j, N_PASS)].rearrange("p (q t) -> p t q", t=PACK),
+                    in1=b1_sorted[:, j],
                     op=ADD,
                 )
                 pre_relu.append(sorted_rows)
@@ -197,6 +210,8 @@ def tile_dpn_kernel(tc, x, W1_words, W1_scales, b1, W2_words, W2_scales, b2, out
         grouped = {}
         for j in range(H_GROUPS):
             pre_relu[j] = first_product(j)
+            if j + 1 < H_GROUPS:
+                spread_bias(j + 1)
             if j >= 1:
                 grouped[j - 1] = turn_and_relu(pre_relu[j - 1])
             if j >= 2:

@@ -52,7 +52,7 @@ def tile_dpn_kernel(tc, x, W1_words, W1_scales, b1, W2_words, W2_scales, b2, out
         w2_words = keep.tile([P, C_GROUPS, D_OUT], U32, align_bytes=64)
         w2_planes = keep.tile([P, W2_SLOTS, D_OUT], U8, align_bytes=64)
         bias_rows = keep.tile([P, N_PASS], BF16)
-        b1_sorted = keep.tile([P, H_GROUPS, PACK, P], BF16)
+        b1_sorted = keep.tile([P, H_GROUPS, 2, P, 2], BF16)
         b2_all = keep.tile([P, D_OUT], BF16)
         c_codes = keep.tile([P, C_GROUPS, BATCH], U32, align_bytes=64)
         c_planes = keep.tile([P, C_GROUPS, BATCH], U8, align_bytes=64)
@@ -113,9 +113,7 @@ def tile_dpn_kernel(tc, x, W1_words, W1_scales, b1, W2_words, W2_scales, b2, out
                 start=True,
                 stop=True,
             )
-            nc.scalar.copy(out=b1_sorted[:, j], in_=spread[:].rearrange("p (q t) -> p t q", t=PACK))
-
-        spread_bias(0)
+            nc.scalar.copy(out=b1_sorted[:, j], in_=spread[:].rearrange("p (q u e) -> p u q e", u=2, e=2))
 
         x_pairs = x_sb[:].bitcast(F32)
         pairs_per_pass = K_PASS // 2
@@ -140,6 +138,8 @@ def tile_dpn_kernel(tc, x, W1_words, W1_scales, b1, W2_words, W2_scales, b2, out
                     in_=x_grouped[:, g, :],
                 )
 
+        spread_bias(0)
+
         def first_product(j):
             pre_relu = []
             for r in range(ROW_TILES):
@@ -154,10 +154,10 @@ def tile_dpn_kernel(tc, x, W1_words, W1_scales, b1, W2_words, W2_scales, b2, out
                         start=(g == 0),
                         stop=(g == X_GROUPS - 1),
                     )
-                sorted_rows = h_stage.tile([P, PACK, P], BF16, tag="sorted_rows")
+                sorted_rows = h_stage.tile([P, 2, P, 2], BF16, tag="sorted_rows")
                 nc.vector.tensor_tensor(
                     out=sorted_rows[:],
-                    in0=sums[:].rearrange("p (q t) -> p t q", t=PACK),
+                    in0=sums[:].rearrange("p (q u e) -> p u q e", u=2, e=2),
                     in1=b1_sorted[:, j],
                     op=ADD,
                 )
@@ -168,15 +168,17 @@ def tile_dpn_kernel(tc, x, W1_words, W1_scales, b1, W2_words, W2_scales, b2, out
             grouped = q_stage.tile([P, BATCH, PACK], BF16, tag="grouped", align_bytes=64)
             rows_per_bank = 2 * P
             for pair in range(ROW_TILES // 2):
-                turned = turn_psum.tile([P, PACK, rows_per_bank], BF16, tag="turn")
+                turned = turn_psum.tile([P, 2, rows_per_bank], F32, tag="turn")
                 for i in range(2):
-                    for t in range(PACK):
+                    for u in range(2):
                         nc.tensor.transpose(
-                            turned[:, t, piece(i, P)], pre_relu[2 * pair + i][:, t, :], ident_bf16[:]
+                            turned[:, u, piece(i, P)],
+                            pre_relu[2 * pair + i][:, u].rearrange("p q e -> p (q e)").bitcast(F32),
+                            ident_f32[:],
                         )
                 nc.scalar.activation(
-                    out=grouped[:, piece(pair, rows_per_bank), :],
-                    in_=turned[:].rearrange("p t b -> p b t"),
+                    out=grouped[:, piece(pair, rows_per_bank), :].rearrange("p b (u e) -> p b u e", e=2),
+                    in_=turned[:].bitcast(BF16).rearrange("p u (b e) -> p b u e", e=2),
                     func=RELU,
                 )
             return grouped

@@ -6,7 +6,6 @@ from concourse.masks import make_identity
 BF16 = mybir.dt.bfloat16
 F32 = mybir.dt.float32
 I32 = mybir.dt.int32
-U32 = mybir.dt.uint32
 U8 = mybir.dt.uint8
 FP8X4 = mybir.dt.float8_e4m3fn_x4
 ADD = mybir.AluOpType.add
@@ -23,7 +22,6 @@ ROW_TILES = BATCH // P
 X_GROUPS = D_IN // K_PASS
 H_GROUPS = HID // K_PASS
 C_GROUPS = X_GROUPS + H_GROUPS
-OUT_HALVES = D_OUT // N_PASS
 SCALE_ROWS = 4
 PLANES = 4
 QUADRANTS = 4
@@ -39,28 +37,29 @@ def tile_dpn_kernel(tc, x, W1_words, W1_scales, b1, W2_words, W2_scales, b2, out
     with ExitStack() as stack:
         stack.enter_context(tc.manual_schedule())
         keep = stack.enter_context(tc.tile_pool(name="keep", bufs=1))
-        x_stage = stack.enter_context(tc.tile_pool(name="x_stage", bufs=2))
-        h_stage = stack.enter_context(tc.tile_pool(name="h_stage", bufs=2 * ROW_TILES))
+        x_stage = stack.enter_context(tc.tile_pool(name="x_stage", bufs=4))
+        w_stage = stack.enter_context(tc.tile_pool(name="w_stage", bufs=8))
+        h_stage = stack.enter_context(tc.tile_pool(name="h_stage", bufs=5))
         q_stage = stack.enter_context(tc.tile_pool(name="q_stage", bufs=3))
         o_stage = stack.enter_context(tc.tile_pool(name="o_stage", bufs=4))
-        sums_psum = stack.enter_context(tc.psum_pool(name="sums_psum", bufs=4))
-        turn_psum = stack.enter_context(tc.psum_pool(name="turn_psum", bufs=4))
+        psum = stack.enter_context(tc.psum_pool(name="psum", bufs=8))
 
         x_sb = keep.tile([P, ROW_TILES, D_IN], BF16)
-        w1_words = keep.tile([P, X_GROUPS, HID], U32, align_bytes=64)
+        w1_words = keep.tile([P, X_GROUPS, HID], I32, align_bytes=64)
+        w1_raw_planes = keep.tile([P, HID], U8, align_bytes=64)
         w1_planes = keep.tile([P, HID], U8, align_bytes=64)
-        w2_words = keep.tile([P, C_GROUPS, D_OUT], U32, align_bytes=64)
+        w2_words = keep.tile([P, C_GROUPS, D_OUT], I32, align_bytes=64)
         w2_planes = keep.tile([P, W2_SLOTS, D_OUT], U8, align_bytes=64)
         bias_rows = keep.tile([P, N_PASS], BF16)
-        b1_sorted = keep.tile([P, H_GROUPS, 2, P, 2], BF16)
+        b1_cols = keep.tile([P, PACK, H_GROUPS], F32)
         b2_all = keep.tile([P, D_OUT], BF16)
-        c_codes = keep.tile([P, C_GROUPS, BATCH], U32, align_bytes=64)
+        c_codes = keep.tile([P, C_GROUPS, BATCH], I32, align_bytes=64)
         c_planes = keep.tile([P, C_GROUPS, BATCH], U8, align_bytes=64)
         ident_f32 = keep.tile([P, P], F32)
         ident_bf16 = keep.tile([P, P], BF16)
 
+        nc.vector.memset(w1_raw_planes[:].bitcast(I32), 0)
         nc.vector.memset(bias_rows[:], 0.0)
-        nc.vector.memset(w1_planes[:].bitcast(I32), 0)
         nc.vector.memset(w2_planes[:].bitcast(I32), 0)
         make_identity(nc, ident_f32[:])
         make_identity(nc, ident_bf16[:])
@@ -68,25 +67,22 @@ def tile_dpn_kernel(tc, x, W1_words, W1_scales, b1, W2_words, W2_scales, b2, out
         nc.scalar.dma_start(out=bias_rows[0:H_GROUPS, :], in_=b1.rearrange("(j n) -> j n", n=N_PASS))
         for r in range(ROW_TILES):
             nc.sync.dma_start(out=x_sb[:, r, :], in_=x[piece(r, P), :])
+        for quad in range(QUADRANTS):
+            first = 32 * quad
+            nc.sync.dma_start(
+                out=w1_raw_planes[first : first + SCALE_ROWS * X_GROUPS, :].bitcast(I32),
+                in_=W1_scales[:, piece(quad, SCALE_ROWS), :].bitcast(I32),
+            )
         w1_by_partition = W1_words.rearrange("g p n t -> p g (n t)")
 
-        def load_w1_piece(j):
+        raw_words = []
+        for j in range(H_GROUPS):
+            raw = w_stage.tile([P, X_GROUPS, N_PASS], I32, tag="raw", align_bytes=64)
             nc.sync.dma_start(
-                out=w1_words[:, :, piece(j, N_PASS)].bitcast(I32),
+                out=raw[:],
                 in_=w1_by_partition[:, :, piece(j, N_PASS * PACK)].bitcast(I32),
             )
-
-        def load_w1_planes():
-            for quad in range(QUADRANTS):
-                first = 32 * quad
-                nc.sync.dma_start(
-                    out=w1_planes[first : first + SCALE_ROWS * X_GROUPS, :].bitcast(I32),
-                    in_=W1_scales[:, piece(quad, SCALE_ROWS), :].bitcast(I32),
-                )
-
-        load_w1_planes()
-        for j in range(H_GROUPS):
-            load_w1_piece(j)
+            raw_words.append(raw)
         for slot in range(W2_SLOTS):
             groups = min(PLANES, C_GROUPS - slot * PLANES)
             for quad in range(QUADRANTS):
@@ -99,26 +95,27 @@ def tile_dpn_kernel(tc, x, W1_words, W1_scales, b1, W2_words, W2_scales, b2, out
                 )
         for g in range(C_GROUPS):
             nc.sync.dma_start(
-                out=w2_words[:, g, :].bitcast(I32),
+                out=w2_words[:, g, :],
                 in_=W2_words[g].rearrange("p n t -> p (n t)").bitcast(I32),
             )
         nc.sync.dma_start(out=b2_all[:], in_=b2.partition_broadcast(P))
 
-        def spread_bias(j):
-            spread = turn_psum.tile([P, N_PASS], F32, tag="turn")
-            nc.tensor.matmul(
-                out=spread[:],
-                lhsT=ident_bf16[:, j : j + 1].to_broadcast([P, P]),
-                rhs=bias_rows[:],
-                start=True,
-                stop=True,
+        def sort_w1_scales(j):
+            nc.vector.tensor_copy(
+                out=w1_planes[:, piece(j, N_PASS)].rearrange("p (t m) -> p t m", t=PACK),
+                in_=w1_raw_planes[:, piece(j, N_PASS)].rearrange("p (m t) -> p t m", t=PACK),
             )
-            nc.scalar.copy(out=b1_sorted[:, j], in_=spread[:].rearrange("p (q u e) -> p u q e", u=2, e=2))
+
+        def sort_w1_words(j):
+            nc.vector.tensor_copy(
+                out=w1_words[:, :, piece(j, N_PASS)].rearrange("p g (t m) -> p g t m", t=PACK),
+                in_=raw_words[j][:].rearrange("p g (m t) -> p g t m", t=PACK),
+            )
 
         x_pairs = x_sb[:].bitcast(F32)
         pairs_per_pass = K_PASS // 2
         for r in range(ROW_TILES):
-            x_turned = turn_psum.tile([P, X_GROUPS, 2, P], F32, tag="turn")
+            x_turned = psum.tile([P, X_GROUPS, 2, P], F32, tag="bank")
             for g in range(X_GROUPS):
                 for u in range(2):
                     nc.tensor.transpose(
@@ -138,49 +135,40 @@ def tile_dpn_kernel(tc, x, W1_words, W1_scales, b1, W2_words, W2_scales, b2, out
                     in_=x_grouped[:, g, :],
                 )
 
-        spread_bias(0)
+        b1_turned = psum.tile([P, PACK, H_GROUPS], F32, tag="bank")
+        for t in range(PACK):
+            nc.tensor.matmul(
+                out=b1_turned[:, t, :],
+                lhsT=bias_rows[:, t : N_PASS : PACK],
+                rhs=ident_bf16[:, 0:H_GROUPS],
+                start=True,
+                stop=True,
+            )
+        nc.scalar.copy(out=b1_cols[:], in_=b1_turned[:])
 
         def first_product(j):
-            pre_relu = []
-            for r in range(ROW_TILES):
-                sums = sums_psum.tile([P, N_PASS], F32, tag="sums")
+            h = h_stage.tile([P, PACK, BATCH], BF16, tag="h")
+            for t in range(PACK):
+                sums = psum.tile([P, BATCH], F32, tag="bank")
+                cols = piece(j * PACK + t, P)
                 for g in range(X_GROUPS):
                     nc.tensor.matmul_mx(
                         out=sums[:],
-                        lhsT=c_codes[:, g, piece(r, P)].bitcast(FP8X4),
-                        lhsT_scale=c_planes[:, g, piece(r, P)],
-                        rhs=w1_words[:, g, piece(j, N_PASS)].bitcast(FP8X4),
-                        rhs_scale=w1_planes[SCALE_ROWS * g : P, piece(j, N_PASS)],
+                        lhsT=w1_words[:, g, cols].bitcast(FP8X4),
+                        lhsT_scale=w1_planes[SCALE_ROWS * g : P, cols],
+                        rhs=c_codes[:, g, :].bitcast(FP8X4),
+                        rhs_scale=c_planes[:, g, :],
                         start=(g == 0),
                         stop=(g == X_GROUPS - 1),
                     )
-                sorted_rows = h_stage.tile([P, 2, P, 2], BF16, tag="sorted_rows")
-                nc.vector.tensor_tensor(
-                    out=sorted_rows[:],
-                    in0=sums[:].rearrange("p (q u e) -> p u q e", u=2, e=2),
-                    in1=b1_sorted[:, j],
-                    op=ADD,
-                )
-                pre_relu.append(sorted_rows)
-            return pre_relu
-
-        def turn_and_relu(pre_relu):
-            grouped = q_stage.tile([P, BATCH, PACK], BF16, tag="grouped", align_bytes=64)
-            rows_per_bank = 2 * P
-            for pair in range(ROW_TILES // 2):
-                turned = turn_psum.tile([P, 2, rows_per_bank], F32, tag="turn")
-                for i in range(2):
-                    for u in range(2):
-                        nc.tensor.transpose(
-                            turned[:, u, piece(i, P)],
-                            pre_relu[2 * pair + i][:, u].rearrange("p q e -> p (q e)").bitcast(F32),
-                            ident_f32[:],
-                        )
                 nc.scalar.activation(
-                    out=grouped[:, piece(pair, rows_per_bank), :].rearrange("p b (u e) -> p b u e", e=2),
-                    in_=turned[:].bitcast(BF16).rearrange("p u (b e) -> p b u e", e=2),
-                    func=RELU,
+                    out=h[:, t, :], in_=sums[:], func=RELU, bias=b1_cols[:, t, j : j + 1]
                 )
+            return h
+
+        def interleave(h):
+            grouped = q_stage.tile([P, BATCH, PACK], BF16, tag="grouped", align_bytes=64)
+            nc.vector.tensor_copy(out=grouped[:], in_=h[:].rearrange("p t b -> p b t"))
             return grouped
 
         def quantise_h(j, grouped):
@@ -190,52 +178,62 @@ def tile_dpn_kernel(tc, x, W1_words, W1_scales, b1, W2_words, W2_scales, b2, out
                 in_=grouped[:].rearrange("p b t -> p (b t)"),
             )
 
-        def second_product_pass(acc, r, half, g):
+        def second_product_pass(acc, r, first_col, width, g):
+            cols = slice(first_col, first_col + width)
             nc.tensor.matmul_mx(
                 out=acc[:],
                 lhsT=c_codes[:, g, piece(r, P)].bitcast(FP8X4),
                 lhsT_scale=c_planes[:, g, piece(r, P)],
-                rhs=w2_words[:, g, piece(half, N_PASS)].bitcast(FP8X4),
-                rhs_scale=w2_planes[SCALE_ROWS * (g % PLANES) : P, g // PLANES, piece(half, N_PASS)],
+                rhs=w2_words[:, g, cols].bitcast(FP8X4),
+                rhs_scale=w2_planes[SCALE_ROWS * (g % PLANES) : P, g // PLANES, cols],
                 start=(g == 0),
                 stop=(g == C_GROUPS - 1),
             )
 
-        def finish(acc, r, half):
-            result = o_stage.tile([P, N_PASS], F32, tag="result")
-            nc.vector.tensor_tensor(
-                out=result[:], in0=acc[:], in1=b2_all[:, piece(half, N_PASS)], op=ADD
-            )
-            nc.sync.dma_start(out=out[piece(r, P), piece(half, N_PASS)], in_=result[:])
+        def finish(acc, r, first_col, width):
+            cols = slice(first_col, first_col + width)
+            result = o_stage.tile([P, width], F32, tag="result%d" % width)
+            nc.vector.tensor_tensor(out=result[:], in0=acc[:], in1=b2_all[:, cols], op=ADD)
+            nc.sync.dma_start(out=out[piece(r, P), cols], in_=result[:])
 
-        pre_relu = {}
-        grouped = {}
+        for j in range(2):
+            sort_w1_scales(j)
+            sort_w1_words(j)
+        h_pieces = []
+        grouped = []
         for j in range(H_GROUPS):
-            pre_relu[j] = first_product(j)
-            if j + 1 < H_GROUPS:
-                spread_bias(j + 1)
-            if j >= 1:
-                grouped[j - 1] = turn_and_relu(pre_relu[j - 1])
-            if j >= 2:
-                quantise_h(j - 2, grouped[j - 2])
+            h_pieces.append(first_product(j))
+            for ahead in range(2 * j + 2, min(2 * j + 4, H_GROUPS)):
+                sort_w1_scales(ahead)
+                sort_w1_words(ahead)
+            if 2 * j + 2 >= H_GROUPS:
+                for done in range(len(grouped), min(len(grouped) + 2, j)):
+                    grouped.append(interleave(h_pieces[done]))
+                    if done >= 1:
+                        quantise_h(done - 1, grouped[done - 1])
 
         left = []
         for r in range(ROW_TILES):
-            acc = sums_psum.tile([P, N_PASS], F32, tag="sums")
+            acc = psum.tile([P, N_PASS], F32, tag="bank")
             left.append(acc)
         for g in range(X_GROUPS):
             for r in range(ROW_TILES):
-                second_product_pass(left[r], r, 0, g)
-        grouped[H_GROUPS - 1] = turn_and_relu(pre_relu[H_GROUPS - 1])
-        quantise_h(H_GROUPS - 2, grouped[H_GROUPS - 2])
+                second_product_pass(left[r], r, 0, N_PASS, g)
+        for done in range(len(grouped), H_GROUPS):
+            grouped.append(interleave(h_pieces[done]))
+            quantise_h(done - 1, grouped[done - 1])
         quantise_h(H_GROUPS - 1, grouped[H_GROUPS - 1])
         for g in range(X_GROUPS, C_GROUPS):
             for r in range(ROW_TILES):
-                second_product_pass(left[r], r, 0, g)
+                second_product_pass(left[r], r, 0, N_PASS, g)
         for r in range(ROW_TILES):
-            finish(left[r], r, 0)
+            finish(left[r], r, 0, N_PASS)
         for r in range(ROW_TILES):
-            acc = turn_psum.tile([P, N_PASS], F32, tag="turn")
-            for g in range(C_GROUPS):
-                second_product_pass(acc, r, 1, g)
-            finish(acc, r, 1)
+            widths = [N_PASS] if r < ROW_TILES - 1 else [N_PASS // 2, N_PASS // 2]
+            first_col = N_PASS
+            for width in widths:
+                acc = psum.tile([P, width], F32, tag="bank")
+                for g in range(C_GROUPS):
+                    second_product_pass(acc, r, first_col, width, g)
+                finish(acc, r, first_col, width)
+                first_col += width

@@ -50,6 +50,7 @@ def tile_dpn_kernel(tc, x, W1_words, W1_scales, b1, W2_words, W2_scales, b2, out
         w1_planes = keep.tile([P, HID], U8, align_bytes=64)
         w2_words = keep.tile([P, C_GROUPS, D_OUT], I32, align_bytes=64)
         w2_planes = keep.tile([P, W2_SLOTS, D_OUT], U8, align_bytes=64)
+        warm = keep.tile([P, 1], F32)
         bias_rows = keep.tile([P, N_PASS], BF16)
         b1_cols = keep.tile([P, PACK, H_GROUPS], F32)
         b2_all = keep.tile([P, D_OUT], BF16)
@@ -58,31 +59,43 @@ def tile_dpn_kernel(tc, x, W1_words, W1_scales, b1, W2_words, W2_scales, b2, out
         ident_f32 = keep.tile([P, P], F32)
         ident_bf16 = keep.tile([P, P], BF16)
 
-        nc.vector.memset(w1_raw_planes[:].bitcast(I32), 0)
+        nc.vector.memset(warm[:], 0.0)
         nc.vector.memset(bias_rows[:], 0.0)
+        nc.vector.memset(w1_raw_planes[:].bitcast(I32), 0)
         nc.vector.memset(w2_planes[:].bitcast(I32), 0)
         make_identity(nc, ident_f32[:])
         make_identity(nc, ident_bf16[:])
 
+        nc.scalar.activation(out=warm[:], in_=warm[:], func=RELU)
         nc.scalar.dma_start(out=bias_rows[0:H_GROUPS, :], in_=b1.rearrange("(j n) -> j n", n=N_PASS))
-        for r in range(ROW_TILES):
-            nc.sync.dma_start(out=x_sb[:, r, :], in_=x[piece(r, P), :])
-        for quad in range(QUADRANTS):
-            first = 32 * quad
-            nc.sync.dma_start(
-                out=w1_raw_planes[first : first + SCALE_ROWS * X_GROUPS, :].bitcast(I32),
-                in_=W1_scales[:, piece(quad, SCALE_ROWS), :].bitcast(I32),
-            )
-        w1_by_partition = W1_words.rearrange("g p n t -> p g (n t)")
 
+        def load_x(r):
+            nc.sync.dma_start(out=x_sb[:, r, :], in_=x[piece(r, P), :])
+
+        w1_by_partition = W1_words.rearrange("g p n t -> p g (n t)")
         raw_words = []
-        for j in range(H_GROUPS):
+
+        def load_w1_piece(j):
             raw = w_stage.tile([P, X_GROUPS, N_PASS], I32, tag="raw", align_bytes=64)
             nc.sync.dma_start(
                 out=raw[:],
                 in_=w1_by_partition[:, :, piece(j, N_PASS * PACK)].bitcast(I32),
             )
             raw_words.append(raw)
+
+        load_x(0)
+        load_x(1)
+        for quad in range(QUADRANTS):
+            first = 32 * quad
+            nc.sync.dma_start(
+                out=w1_raw_planes[first : first + SCALE_ROWS * X_GROUPS, :].bitcast(I32),
+                in_=W1_scales[:, piece(quad, SCALE_ROWS), :].bitcast(I32),
+            )
+        load_w1_piece(0)
+        load_x(2)
+        load_x(3)
+        for j in range(1, H_GROUPS):
+            load_w1_piece(j)
         for slot in range(W2_SLOTS):
             groups = min(PLANES, C_GROUPS - slot * PLANES)
             for quad in range(QUADRANTS):
@@ -128,6 +141,9 @@ def tile_dpn_kernel(tc, x, W1_words, W1_scales, b1, W2_words, W2_scales, b2, out
                 out=x_grouped[:].bitcast(F32).rearrange("p g (b u) -> p g b u", u=2),
                 in_=x_turned[:].rearrange("p g u b -> p g b u"),
             )
+            if r == ROW_TILES // 2:
+                sort_w1_scales(0)
+                sort_w1_words(0)
             for g in range(X_GROUPS):
                 nc.vector.quantize_mx(
                     out=c_codes[:, g, piece(r, P)].bitcast(FP8X4),
@@ -148,22 +164,28 @@ def tile_dpn_kernel(tc, x, W1_words, W1_scales, b1, W2_words, W2_scales, b2, out
 
         def first_product(j):
             h = h_stage.tile([P, PACK, BATCH], BF16, tag="h")
+            banks = []
             for t in range(PACK):
                 sums = psum.tile([P, BATCH], F32, tag="bank")
-                cols = piece(j * PACK + t, P)
-                for g in range(X_GROUPS):
-                    nc.tensor.matmul_mx(
-                        out=sums[:],
-                        lhsT=w1_words[:, g, cols].bitcast(FP8X4),
-                        lhsT_scale=w1_planes[SCALE_ROWS * g : P, cols],
-                        rhs=c_codes[:, g, :].bitcast(FP8X4),
-                        rhs_scale=c_planes[:, g, :],
-                        start=(g == 0),
-                        stop=(g == X_GROUPS - 1),
+                banks.append(sums)
+            parts = 2 if j == 0 else 1
+            for part in range(parts):
+                rows = piece(part, BATCH // parts)
+                for t in range(PACK):
+                    cols = piece(j * PACK + t, P)
+                    for g in range(X_GROUPS):
+                        nc.tensor.matmul_mx(
+                            out=banks[t][:, rows],
+                            lhsT=w1_words[:, g, cols].bitcast(FP8X4),
+                            lhsT_scale=w1_planes[SCALE_ROWS * g : P, cols],
+                            rhs=c_codes[:, g, rows].bitcast(FP8X4),
+                            rhs_scale=c_planes[:, g, rows],
+                            start=(g == 0),
+                            stop=(g == X_GROUPS - 1),
+                        )
+                    nc.scalar.activation(
+                        out=h[:, t, rows], in_=banks[t][:, rows], func=RELU, bias=b1_cols[:, t, j : j + 1]
                     )
-                nc.scalar.activation(
-                    out=h[:, t, :], in_=sums[:], func=RELU, bias=b1_cols[:, t, j : j + 1]
-                )
             return h
 
         def interleave(h):
@@ -196,9 +218,8 @@ def tile_dpn_kernel(tc, x, W1_words, W1_scales, b1, W2_words, W2_scales, b2, out
             nc.vector.tensor_tensor(out=result[:], in0=acc[:], in1=b2_all[:, cols], op=ADD)
             nc.sync.dma_start(out=out[piece(r, P), cols], in_=result[:])
 
-        for j in range(2):
-            sort_w1_scales(j)
-            sort_w1_words(j)
+        sort_w1_scales(1)
+        sort_w1_words(1)
         h_pieces = []
         grouped = []
         for j in range(H_GROUPS):

@@ -59,9 +59,12 @@ def tile_dpn_kernel(tc, x, W1_words, W1_scales, b1, W2_words, W2_scales, b2, out
         ident_f32 = keep.tile([P, P], F32)
         ident_bf16 = keep.tile([P, P], BF16)
 
+        early_cols = slice(0, 2 * N_PASS)
+        late_cols = slice(2 * N_PASS, HID)
+        nc.vector.memset(w1_raw_planes[:, early_cols].bitcast(I32), 0)
         nc.vector.memset(warm[:], 0.0)
         nc.vector.memset(bias_rows[:], 0.0)
-        nc.vector.memset(w1_raw_planes[:].bitcast(I32), 0)
+        nc.vector.memset(w1_raw_planes[:, late_cols].bitcast(I32), 0)
         nc.vector.memset(w2_planes[:].bitcast(I32), 0)
         make_identity(nc, ident_f32[:])
         make_identity(nc, ident_bf16[:])
@@ -83,18 +86,23 @@ def tile_dpn_kernel(tc, x, W1_words, W1_scales, b1, W2_words, W2_scales, b2, out
             )
             raw_words.append(raw)
 
+        def load_w1_scales(cols):
+            for quad in range(QUADRANTS):
+                first = 32 * quad
+                nc.sync.dma_start(
+                    out=w1_raw_planes[first : first + SCALE_ROWS * X_GROUPS, cols].bitcast(I32),
+                    in_=W1_scales[:, piece(quad, SCALE_ROWS), cols].bitcast(I32),
+                )
+
+        load_w1_scales(early_cols)
         load_x(0)
         load_x(1)
-        for quad in range(QUADRANTS):
-            first = 32 * quad
-            nc.sync.dma_start(
-                out=w1_raw_planes[first : first + SCALE_ROWS * X_GROUPS, :].bitcast(I32),
-                in_=W1_scales[:, piece(quad, SCALE_ROWS), :].bitcast(I32),
-            )
         load_w1_piece(0)
         load_x(2)
         load_x(3)
-        for j in range(1, H_GROUPS):
+        load_w1_piece(1)
+        load_w1_scales(late_cols)
+        for j in range(2, H_GROUPS):
             load_w1_piece(j)
         for slot in range(W2_SLOTS):
             groups = min(PLANES, C_GROUPS - slot * PLANES)

@@ -51,6 +51,7 @@ def tile_dpn_kernel(tc, x, W1_words, W1_scales, b1, W2_words, W2_scales, b2, out
         w2_words = keep.tile([P, C_GROUPS, D_OUT], I32, align_bytes=64)
         w2_planes = keep.tile([P, W2_SLOTS, D_OUT], U8, align_bytes=64)
         warm = keep.tile([P, 1], F32)
+        zeros = keep.tile([P, N_PASS], BF16)
         bias_rows = keep.tile([P, N_PASS], BF16)
         b1_cols = keep.tile([P, PACK, H_GROUPS], F32)
         b2_all = keep.tile([P, D_OUT], BF16)
@@ -62,6 +63,7 @@ def tile_dpn_kernel(tc, x, W1_words, W1_scales, b1, W2_words, W2_scales, b2, out
         early_cols = slice(0, 2 * N_PASS)
         late_cols = slice(2 * N_PASS, HID)
         nc.vector.memset(w1_raw_planes[:, early_cols].bitcast(I32), 0)
+        nc.vector.memset(zeros[:], 0.0)
         nc.vector.memset(warm[:], 0.0)
         nc.vector.memset(bias_rows[:], 0.0)
         nc.vector.memset(w1_raw_planes[:, late_cols].bitcast(I32), 0)
@@ -135,7 +137,16 @@ def tile_dpn_kernel(tc, x, W1_words, W1_scales, b1, W2_words, W2_scales, b2, out
 
         x_pairs = x_sb[:].bitcast(F32)
         pairs_per_pass = K_PASS // 2
+        idle_bank = psum.tile([P, N_PASS], F32, tag="bank")
+
+        def keep_warm(count):
+            for i in range(count):
+                nc.tensor.matmul(out=idle_bank[:], lhsT=zeros[:, 0:P], rhs=zeros[:], start=True, stop=True)
+
+        keep_warm(6)
         for r in range(ROW_TILES):
+            if r == ROW_TILES // 2:
+                keep_warm(2)
             x_turned = psum.tile([P, X_GROUPS, 2, P], F32, tag="bank")
             for g in range(X_GROUPS):
                 for u in range(2):
@@ -169,6 +180,7 @@ def tile_dpn_kernel(tc, x, W1_words, W1_scales, b1, W2_words, W2_scales, b2, out
                 stop=True,
             )
         nc.scalar.copy(out=b1_cols[:], in_=b1_turned[:])
+        keep_warm(3)
 
         def first_product(j):
             h = h_stage.tile([P, PACK, BATCH], BF16, tag="h")

@@ -45,18 +45,18 @@ def tile_dpn_kernel(tc, x, W1_words, W1_scales, b1, W2_words, W2_scales, b2, out
         psum = stack.enter_context(tc.psum_pool(name="psum", bufs=8))
 
         x_sb = keep.tile([P, ROW_TILES, D_IN], BF16)
-        w1_words = keep.tile([P, X_GROUPS, HID], I32, align_bytes=64)
-        w1_raw_planes = keep.tile([P, HID], U8, align_bytes=64)
-        w1_planes = keep.tile([P, HID], U8, align_bytes=64)
-        w2_words = keep.tile([P, C_GROUPS, D_OUT], I32, align_bytes=64)
-        w2_planes = keep.tile([P, W2_SLOTS, D_OUT], U8, align_bytes=64)
+        w1_words = keep.tile([P, X_GROUPS, HID], I32, align_bytes=256)
+        w1_raw_planes = keep.tile([P, HID], U8, align_bytes=256)
+        w1_planes = keep.tile([P, HID], U8, align_bytes=256)
+        w2_words = keep.tile([P, C_GROUPS, D_OUT], I32, align_bytes=256)
+        w2_planes = keep.tile([P, W2_SLOTS, D_OUT], U8, align_bytes=256)
         warm = keep.tile([P, 1], F32)
         zeros = keep.tile([P, N_PASS], BF16)
         bias_rows = keep.tile([P, N_PASS], BF16)
         b1_cols = keep.tile([P, PACK, H_GROUPS], F32)
         b2_all = keep.tile([P, D_OUT], BF16)
-        c_codes = keep.tile([P, C_GROUPS, BATCH], I32, align_bytes=64)
-        c_planes = keep.tile([P, C_GROUPS, BATCH], U8, align_bytes=64)
+        c_codes = keep.tile([P, C_GROUPS, BATCH], I32, align_bytes=256)
+        c_planes = keep.tile([P, C_GROUPS, BATCH], U8, align_bytes=256)
         ident_f32 = keep.tile([P, P], F32)
         ident_bf16 = keep.tile([P, P], BF16)
 
@@ -81,7 +81,7 @@ def tile_dpn_kernel(tc, x, W1_words, W1_scales, b1, W2_words, W2_scales, b2, out
         raw_words = []
 
         def load_w1_piece(j):
-            raw = w_stage.tile([P, X_GROUPS, N_PASS], I32, tag="raw", align_bytes=64)
+            raw = w_stage.tile([P, X_GROUPS, N_PASS], I32, tag="raw", align_bytes=256)
             nc.sync.dma_start(
                 out=raw[:],
                 in_=w1_by_partition[:, :, piece(j, N_PASS * PACK)].bitcast(I32),
@@ -155,7 +155,7 @@ def tile_dpn_kernel(tc, x, W1_words, W1_scales, b1, W2_words, W2_scales, b2, out
                         x_pairs[:, r, g * pairs_per_pass + u : (g + 1) * pairs_per_pass : 2],
                         ident_f32[:],
                     )
-            x_grouped = x_stage.tile([P, X_GROUPS, P * PACK], BF16, align_bytes=64)
+            x_grouped = x_stage.tile([P, X_GROUPS, P * PACK], BF16, align_bytes=256)
             nc.scalar.copy(
                 out=x_grouped[:].bitcast(F32).rearrange("p g (b u) -> p g b u", u=2),
                 in_=x_turned[:].rearrange("p g u b -> p g b u"),
@@ -209,7 +209,7 @@ def tile_dpn_kernel(tc, x, W1_words, W1_scales, b1, W2_words, W2_scales, b2, out
             return h
 
         def interleave(h):
-            grouped = q_stage.tile([P, BATCH, PACK], BF16, tag="grouped", align_bytes=64)
+            grouped = q_stage.tile([P, BATCH, PACK], BF16, tag="grouped", align_bytes=256)
             nc.vector.tensor_copy(out=grouped[:], in_=h[:].rearrange("p t b -> p b t"))
             return grouped
 

@@ -125,14 +125,14 @@ def tile_dpn_kernel(tc, x, W1_words, W1_scales, b1, W2_words, W2_scales, b2, out
 
         def sort_w1_scales(j):
             nc.vector.tensor_copy(
-                out=w1_planes[:, piece(j, N_PASS)].rearrange("p (t m) -> p t m", t=PACK),
-                in_=w1_raw_planes[:, piece(j, N_PASS)].rearrange("p (m t) -> p t m", t=PACK),
+                out=w1_planes[:, piece(j, N_PASS)].rearrange("p (t m) -> p m t", t=PACK),
+                in_=w1_raw_planes[:, piece(j, N_PASS)].rearrange("p (m t) -> p m t", t=PACK),
             )
 
         def sort_w1_words(j):
             nc.vector.tensor_copy(
-                out=w1_words[:, :, piece(j, N_PASS)].rearrange("p g (t m) -> p g t m", t=PACK),
-                in_=raw_words[j][:].rearrange("p g (m t) -> p g t m", t=PACK),
+                out=w1_words[:, :, piece(j, N_PASS)].rearrange("p g (t m) -> p g m t", t=PACK),
+                in_=raw_words[j][:].rearrange("p g (m t) -> p g m t", t=PACK),
             )
 
         x_pairs = x_sb[:].bitcast(F32)

@@ -9,6 +9,7 @@ I32 = mybir.dt.int32
 U8 = mybir.dt.uint8
 FP8X4 = mybir.dt.float8_e4m3fn_x4
 ADD = mybir.AluOpType.add
+MAX = mybir.AluOpType.max
 RELU = mybir.ActivationFunctionType.Relu
 
 BATCH, D_IN, HID, D_OUT = 512, 1024, 4096, 1024
@@ -96,8 +97,8 @@ def tile_dpn_kernel(tc, x, W1_words, W1_scales, b1, W2_words, W2_scales, b2, out
                     in_=W1_scales[:, piece(quad, SCALE_ROWS), cols].bitcast(I32),
                 )
 
-        load_w1_scales(early_cols)
         load_x(0)
+        load_w1_scales(early_cols)
         load_x(1)
         load_w1_piece(0)
         load_x(2)
@@ -143,10 +144,7 @@ def tile_dpn_kernel(tc, x, W1_words, W1_scales, b1, W2_words, W2_scales, b2, out
             for i in range(count):
                 nc.tensor.matmul(out=idle_bank[:], lhsT=zeros[:, 0:P], rhs=zeros[:], start=True, stop=True)
 
-        keep_warm(6)
-        for r in range(ROW_TILES):
-            if r == ROW_TILES // 2:
-                keep_warm(2)
+        def turn_x(r):
             x_turned = psum.tile([P, X_GROUPS, 2, P], F32, tag="bank")
             for g in range(X_GROUPS):
                 for u in range(2):
@@ -155,14 +153,14 @@ def tile_dpn_kernel(tc, x, W1_words, W1_scales, b1, W2_words, W2_scales, b2, out
                         x_pairs[:, r, g * pairs_per_pass + u : (g + 1) * pairs_per_pass : 2],
                         ident_f32[:],
                     )
-            x_grouped = x_stage.tile([P, X_GROUPS, P * PACK], BF16, align_bytes=256)
+            x_grouped = x_stage.tile([P, X_GROUPS, P * PACK], BF16, tag="x_grouped", align_bytes=256)
             nc.scalar.copy(
                 out=x_grouped[:].bitcast(F32).rearrange("p g (b u) -> p g b u", u=2),
                 in_=x_turned[:].rearrange("p g u b -> p g b u"),
             )
-            if r == ROW_TILES // 2:
-                sort_w1_scales(0)
-                sort_w1_words(0)
+            return x_grouped
+
+        def quantise_x(r, x_grouped):
             for g in range(X_GROUPS):
                 nc.vector.quantize_mx(
                     out=c_codes[:, g, piece(r, P)].bitcast(FP8X4),
@@ -170,43 +168,51 @@ def tile_dpn_kernel(tc, x, W1_words, W1_scales, b1, W2_words, W2_scales, b2, out
                     in_=x_grouped[:, g, :],
                 )
 
-        b1_turned = psum.tile([P, PACK, H_GROUPS], F32, tag="bank")
-        for t in range(PACK):
-            nc.tensor.matmul(
-                out=b1_turned[:, t, :],
-                lhsT=bias_rows[:, t : N_PASS : PACK],
-                rhs=ident_bf16[:, 0:H_GROUPS],
-                start=True,
-                stop=True,
-            )
-        nc.scalar.copy(out=b1_cols[:], in_=b1_turned[:])
-        keep_warm(3)
+        def turn_b1():
+            b1_turned = psum.tile([P, PACK, H_GROUPS], F32, tag="bank")
+            for t in range(PACK):
+                nc.tensor.matmul(
+                    out=b1_turned[:, t, :],
+                    lhsT=bias_rows[:, t : N_PASS : PACK],
+                    rhs=ident_bf16[:, 0:H_GROUPS],
+                    start=True,
+                    stop=True,
+                )
+            nc.scalar.copy(out=b1_cols[:], in_=b1_turned[:])
 
-        def first_product(j):
+        def open_piece():
             h = h_stage.tile([P, PACK, BATCH], BF16, tag="h")
             banks = []
             for t in range(PACK):
                 sums = psum.tile([P, BATCH], F32, tag="bank")
                 banks.append(sums)
-            parts = 2 if j == 0 else 1
-            for part in range(parts):
-                rows = piece(part, BATCH // parts)
-                for t in range(PACK):
-                    cols = piece(j * PACK + t, P)
-                    for g in range(X_GROUPS):
-                        nc.tensor.matmul_mx(
-                            out=banks[t][:, rows],
-                            lhsT=w1_words[:, g, cols].bitcast(FP8X4),
-                            lhsT_scale=w1_planes[SCALE_ROWS * g : P, cols],
-                            rhs=c_codes[:, g, rows].bitcast(FP8X4),
-                            rhs_scale=c_planes[:, g, rows],
-                            start=(g == 0),
-                            stop=(g == X_GROUPS - 1),
-                        )
-                    nc.scalar.activation(
-                        out=h[:, t, rows], in_=banks[t][:, rows], func=RELU, bias=b1_cols[:, t, j : j + 1]
-                    )
-            return h
+            return h, banks
+
+        def first_product(j, h, banks, t, rows):
+            cols = piece(j * PACK + t, P)
+            for g in range(X_GROUPS):
+                nc.tensor.matmul_mx(
+                    out=banks[t][:, rows],
+                    lhsT=w1_words[:, g, cols].bitcast(FP8X4),
+                    lhsT_scale=w1_planes[SCALE_ROWS * g : P, cols],
+                    rhs=c_codes[:, g, rows].bitcast(FP8X4),
+                    rhs_scale=c_planes[:, g, rows],
+                    start=(g == 0),
+                    stop=(g == X_GROUPS - 1),
+                )
+            if t == 0 and 2 * j + 2 > H_GROUPS - 2:
+                nc.vector.tensor_scalar(
+                    out=h[:, t, rows],
+                    in0=banks[t][:, rows],
+                    scalar1=b1_cols[:, t, j : j + 1],
+                    scalar2=0.0,
+                    op0=ADD,
+                    op1=MAX,
+                )
+            else:
+                nc.scalar.activation(
+                    out=h[:, t, rows], in_=banks[t][:, rows], func=RELU, bias=b1_cols[:, t, j : j + 1]
+                )
 
         def interleave(h):
             grouped = q_stage.tile([P, BATCH, PACK], BF16, tag="grouped", align_bytes=256)
@@ -238,12 +244,38 @@ def tile_dpn_kernel(tc, x, W1_words, W1_scales, b1, W2_words, W2_scales, b2, out
             nc.vector.tensor_tensor(out=result[:], in0=acc[:], in1=b2_all[:, cols], op=ADD)
             nc.sync.dma_start(out=out[piece(r, P), cols], in_=result[:])
 
-        sort_w1_scales(1)
-        sort_w1_words(1)
+        def first_piece():
+            early, late = piece(0, BATCH // 2), piece(1, BATCH // 2)
+            keep_warm(4)
+            sort_w1_scales(0)
+            sort_w1_scales(1)
+            quantise_x(0, turn_x(0))
+            sort_w1_words(0)
+            quantise_x(1, turn_x(1))
+            keep_warm(1)
+            quantise_x(2, turn_x(2))
+            turn_b1()
+            h, banks = open_piece()
+            for t in range(PACK // 2):
+                first_product(0, h, banks, t, early)
+            quantise_x(3, turn_x(3))
+            for t in range(PACK // 2, PACK):
+                first_product(0, h, banks, t, early)
+            for t in range(PACK):
+                first_product(0, h, banks, t, late)
+            return h
+
         h_pieces = []
         grouped = []
         for j in range(H_GROUPS):
-            h_pieces.append(first_product(j))
+            if j == 0:
+                h_pieces.append(first_piece())
+                sort_w1_words(1)
+            else:
+                h, banks = open_piece()
+                for t in range(PACK):
+                    first_product(j, h, banks, t, slice(0, BATCH))
+                h_pieces.append(h)
             for ahead in range(2 * j + 2, min(2 * j + 4, H_GROUPS)):
                 sort_w1_scales(ahead)
                 sort_w1_words(ahead)
@@ -270,7 +302,7 @@ def tile_dpn_kernel(tc, x, W1_words, W1_scales, b1, W2_words, W2_scales, b2, out
         for r in range(ROW_TILES):
             finish(left[r], r, 0, N_PASS)
         for r in range(ROW_TILES):
-            widths = [N_PASS] if r < ROW_TILES - 1 else [N_PASS // 2, N_PASS // 2]
+            widths = [N_PASS] if r < ROW_TILES - 1 else [N_PASS // 2, N_PASS // 4, N_PASS // 4]
             first_col = N_PASS
             for width in widths:
                 acc = psum.tile([P, width], F32, tag="bank")

@@ -145,19 +145,21 @@ def tile_dpn_kernel(tc, x, W1_words, W1_scales, b1, W2_words, W2_scales, b2, out
                 nc.tensor.matmul(out=idle_bank[:], lhsT=zeros[:, 0:P], rhs=zeros[:], start=True, stop=True)
 
         def turn_x(r):
-            x_turned = psum.tile([P, X_GROUPS, 2, P], F32, tag="bank")
+            x_grouped = x_stage.tile([P, X_GROUPS, P * PACK], BF16, tag="x_grouped", align_bytes=256)
             for g in range(X_GROUPS):
+                x_turned = psum.tile([P, 2, P], F32, tag="bank")
                 for u in range(2):
                     nc.tensor.transpose(
-                        x_turned[:, g, u, :],
+                        x_turned[:, u, :],
                         x_pairs[:, r, g * pairs_per_pass + u : (g + 1) * pairs_per_pass : 2],
                         ident_f32[:],
                     )
-            x_grouped = x_stage.tile([P, X_GROUPS, P * PACK], BF16, tag="x_grouped", align_bytes=256)
-            nc.scalar.copy(
-                out=x_grouped[:].bitcast(F32).rearrange("p g (b u) -> p g b u", u=2),
-                in_=x_turned[:].rearrange("p g u b -> p g b u"),
-            )
+                grouped = x_grouped[:, g, :].bitcast(F32).rearrange("p (b u) -> p b u", u=2)
+                turned = x_turned[:].rearrange("p u b -> p b u")
+                if g == 0:
+                    nc.scalar.copy(out=grouped, in_=turned)
+                else:
+                    nc.vector.tensor_copy(out=grouped, in_=turned)
             return x_grouped
 
         def quantise_x(r, x_grouped):
@@ -188,7 +190,7 @@ def tile_dpn_kernel(tc, x, W1_words, W1_scales, b1, W2_words, W2_scales, b2, out
                 banks.append(sums)
             return h, banks
 
-        def first_product(j, h, banks, t, rows):
+        def multiply(j, banks, t, rows):
             cols = piece(j * PACK + t, P)
             for g in range(X_GROUPS):
                 nc.tensor.matmul_mx(
@@ -200,6 +202,7 @@ def tile_dpn_kernel(tc, x, W1_words, W1_scales, b1, W2_words, W2_scales, b2, out
                     start=(g == 0),
                     stop=(g == X_GROUPS - 1),
                 )
+        def add_and_relu(j, h, banks, t, rows):
             if t == 0 and 2 * j + 2 > H_GROUPS - 2:
                 nc.vector.tensor_scalar(
                     out=h[:, t, rows],
@@ -246,23 +249,32 @@ def tile_dpn_kernel(tc, x, W1_words, W1_scales, b1, W2_words, W2_scales, b2, out
 
         def first_piece():
             early, late = piece(0, BATCH // 2), piece(1, BATCH // 2)
-            keep_warm(4)
+            keep_warm(6)
             sort_w1_scales(0)
             sort_w1_scales(1)
-            quantise_x(0, turn_x(0))
+            x0 = turn_x(0)
+            x1 = turn_x(1)
+            quantise_x(0, x0)
+            quantise_x(1, x1)
             sort_w1_words(0)
-            quantise_x(1, turn_x(1))
-            keep_warm(1)
-            quantise_x(2, turn_x(2))
+            keep_warm(2)
+            x2 = turn_x(2)
             turn_b1()
+            keep_warm(1)
             h, banks = open_piece()
             for t in range(PACK // 2):
-                first_product(0, h, banks, t, early)
-            quantise_x(3, turn_x(3))
+                multiply(0, banks, t, early)
+            x3 = turn_x(3)
+            quantise_x(2, x2)
+            quantise_x(3, x3)
+            for t in range(PACK // 2):
+                add_and_relu(0, h, banks, t, early)
             for t in range(PACK // 2, PACK):
-                first_product(0, h, banks, t, early)
+                multiply(0, banks, t, early)
+                add_and_relu(0, h, banks, t, early)
             for t in range(PACK):
-                first_product(0, h, banks, t, late)
+                multiply(0, banks, t, late)
+                add_and_relu(0, h, banks, t, late)
             return h
 
         h_pieces = []
@@ -274,7 +286,8 @@ def tile_dpn_kernel(tc, x, W1_words, W1_scales, b1, W2_words, W2_scales, b2, out
             else:
                 h, banks = open_piece()
                 for t in range(PACK):
-                    first_product(j, h, banks, t, slice(0, BATCH))
+                    multiply(j, banks, t, slice(0, BATCH))
+                    add_and_relu(j, h, banks, t, slice(0, BATCH))
                 h_pieces.append(h)
             for ahead in range(2 * j + 2, min(2 * j + 4, H_GROUPS)):
                 sort_w1_scales(ahead)

@@ -9,7 +9,6 @@ I32 = mybir.dt.int32
 U8 = mybir.dt.uint8
 FP8X4 = mybir.dt.float8_e4m3fn_x4
 ADD = mybir.AluOpType.add
-MAX = mybir.AluOpType.max
 RELU = mybir.ActivationFunctionType.Relu
 
 BATCH, D_IN, HID, D_OUT = 512, 1024, 4096, 1024
@@ -203,23 +202,16 @@ def tile_dpn_kernel(tc, x, W1_words, W1_scales, b1, W2_words, W2_scales, b2, out
                     stop=(g == X_GROUPS - 1),
                 )
         def add_and_relu(j, h, banks, t, rows):
-            if t == 0 and 2 * j + 2 > H_GROUPS - 2:
-                nc.vector.tensor_scalar(
-                    out=h[:, t, rows],
-                    in0=banks[t][:, rows],
-                    scalar1=b1_cols[:, t, j : j + 1],
-                    scalar2=0.0,
-                    op0=ADD,
-                    op1=MAX,
-                )
-            else:
-                nc.scalar.activation(
-                    out=h[:, t, rows], in_=banks[t][:, rows], func=RELU, bias=b1_cols[:, t, j : j + 1]
-                )
+            nc.scalar.activation(
+                out=h[:, t, rows], in_=banks[t][:, rows], func=RELU, bias=b1_cols[:, t, j : j + 1]
+            )
 
         def interleave(h):
             grouped = q_stage.tile([P, BATCH, PACK], BF16, tag="grouped", align_bytes=256)
-            nc.vector.tensor_copy(out=grouped[:], in_=h[:].rearrange("p t b -> p b t"))
+            nc.vector.tensor_copy(
+                out=grouped[:].rearrange("p (c i) t -> p c t i", i=4),
+                in_=h[:].rearrange("p t (c i) -> p c t i", i=4),
+            )
             return grouped
 
         def quantise_h(j, grouped):
@@ -302,9 +294,16 @@ def tile_dpn_kernel(tc, x, W1_words, W1_scales, b1, W2_words, W2_scales, b2, out
         for r in range(ROW_TILES):
             acc = psum.tile([P, N_PASS], F32, tag="bank")
             left.append(acc)
+        right = []
+        for r in range(ROW_TILES - 1):
+            acc = psum.tile([P, N_PASS], F32, tag="bank")
+            right.append(acc)
         for g in range(X_GROUPS):
             for r in range(ROW_TILES):
                 second_product_pass(left[r], r, 0, N_PASS, g)
+        for r in range(ROW_TILES - 1):
+            for g in range(X_GROUPS):
+                second_product_pass(right[r], r, N_PASS, N_PASS, g)
         for done in range(len(grouped), H_GROUPS):
             grouped.append(interleave(h_pieces[done]))
             quantise_h(done - 1, grouped[done - 1])
@@ -314,12 +313,14 @@ def tile_dpn_kernel(tc, x, W1_words, W1_scales, b1, W2_words, W2_scales, b2, out
                 second_product_pass(left[r], r, 0, N_PASS, g)
         for r in range(ROW_TILES):
             finish(left[r], r, 0, N_PASS)
-        for r in range(ROW_TILES):
-            widths = [N_PASS] if r < ROW_TILES - 1 else [N_PASS // 2, N_PASS // 4, N_PASS // 4]
-            first_col = N_PASS
-            for width in widths:
-                acc = psum.tile([P, width], F32, tag="bank")
-                for g in range(C_GROUPS):
-                    second_product_pass(acc, r, first_col, width, g)
-                finish(acc, r, first_col, width)
-                first_col += width
+        for r in range(ROW_TILES - 1):
+            for g in range(X_GROUPS, C_GROUPS):
+                second_product_pass(right[r], r, N_PASS, N_PASS, g)
+            finish(right[r], r, N_PASS, N_PASS)
+        first_col = N_PASS
+        for width in [N_PASS // 2, N_PASS // 4, N_PASS // 4]:
+            acc = psum.tile([P, width], F32, tag="bank")
+            for g in range(C_GROUPS):
+                second_product_pass(acc, ROW_TILES - 1, first_col, width, g)
+            finish(acc, ROW_TILES - 1, first_col, width)
+            first_col += width

@@ -74,8 +74,11 @@ def tile_dpn_kernel(tc, x, W1_words, W1_scales, b1, W2_words, W2_scales, b2, out
         nc.scalar.activation(out=warm[:], in_=warm[:], func=RELU)
         nc.scalar.dma_start(out=bias_rows[0:H_GROUPS, :], in_=b1.rearrange("(j n) -> j n", n=N_PASS))
 
-        def load_x(r):
-            nc.sync.dma_start(out=x_sb[:, r, :], in_=x[piece(r, P), :])
+        x_by_tile = x.rearrange("(r p) d -> p r d", p=P)
+
+        def load_x(first, count):
+            tiles = slice(first, first + count)
+            nc.sync.dma_start(out=x_sb[:, tiles, :], in_=x_by_tile[:, tiles, :])
 
         w1_by_partition = W1_words.rearrange("g p n t -> p g (n t)")
         raw_words = []
@@ -96,12 +99,11 @@ def tile_dpn_kernel(tc, x, W1_words, W1_scales, b1, W2_words, W2_scales, b2, out
                     in_=W1_scales[:, piece(quad, SCALE_ROWS), cols].bitcast(I32),
                 )
 
-        load_x(0)
+        load_x(0, 2)
         load_w1_scales(early_cols)
-        load_x(1)
         load_w1_piece(0)
-        load_x(2)
-        load_x(3)
+        load_x(2, 1)
+        load_x(3, 1)
         load_w1_piece(1)
         load_w1_scales(late_cols)
         for j in range(2, H_GROUPS):
@@ -241,7 +243,7 @@ def tile_dpn_kernel(tc, x, W1_words, W1_scales, b1, W2_words, W2_scales, b2, out
 
         def first_piece():
             early, late = piece(0, BATCH // 2), piece(1, BATCH // 2)
-            keep_warm(6)
+            keep_warm(4)
             sort_w1_scales(0)
             sort_w1_scales(1)
             x0 = turn_x(0)
@@ -251,17 +253,12 @@ def tile_dpn_kernel(tc, x, W1_words, W1_scales, b1, W2_words, W2_scales, b2, out
             sort_w1_words(0)
             keep_warm(2)
             x2 = turn_x(2)
-            turn_b1()
-            keep_warm(1)
-            h, banks = open_piece()
-            for t in range(PACK // 2):
-                multiply(0, banks, t, early)
             x3 = turn_x(3)
+            turn_b1()
             quantise_x(2, x2)
             quantise_x(3, x3)
-            for t in range(PACK // 2):
-                add_and_relu(0, h, banks, t, early)
-            for t in range(PACK // 2, PACK):
+            h, banks = open_piece()
+            for t in range(PACK):
                 multiply(0, banks, t, early)
                 add_and_relu(0, h, banks, t, early)
             for t in range(PACK):

from contextlib import ExitStack

import concourse.mybir as mybir
from concourse.masks import make_identity

BF16 = mybir.dt.bfloat16
F32 = mybir.dt.float32
I32 = mybir.dt.int32
U8 = mybir.dt.uint8
FP8X4 = mybir.dt.float8_e4m3fn_x4
ADD = mybir.AluOpType.add
RELU = mybir.ActivationFunctionType.Relu

BATCH, D_IN, HID, D_OUT = 512, 1024, 4096, 1024
FLOPS = 2 * BATCH * D_IN * HID + 2 * BATCH * (D_IN + HID) * D_OUT

P = 128
PACK = 4
K_PASS = P * PACK
N_PASS = 512
ROW_TILES = BATCH // P
X_GROUPS = D_IN // K_PASS
H_GROUPS = HID // K_PASS
C_GROUPS = X_GROUPS + H_GROUPS
SCALE_ROWS = 4
PLANES = 4
QUADRANTS = 4
W2_SLOTS = (C_GROUPS + PLANES - 1) // PLANES


def piece(i, width):
    return slice(i * width, (i + 1) * width)


def tile_dpn_kernel(tc, x, W1_words, W1_scales, b1, W2_words, W2_scales, b2, out):
    nc = tc.nc
    with ExitStack() as stack:
        stack.enter_context(tc.manual_schedule())
        keep = stack.enter_context(tc.tile_pool(name="keep", bufs=1))
        x_stage = stack.enter_context(tc.tile_pool(name="x_stage", bufs=4))
        w_stage = stack.enter_context(tc.tile_pool(name="w_stage", bufs=8))
        h_stage = stack.enter_context(tc.tile_pool(name="h_stage", bufs=5))
        q_stage = stack.enter_context(tc.tile_pool(name="q_stage", bufs=3))
        o_stage = stack.enter_context(tc.tile_pool(name="o_stage", bufs=4))
        psum = stack.enter_context(tc.psum_pool(name="psum", bufs=8))

        x_sb = keep.tile([P, ROW_TILES, D_IN], BF16)
        w1_words = keep.tile([P, X_GROUPS, HID], I32, align_bytes=256)
        w1_raw_planes = keep.tile([P, HID], U8, align_bytes=256)
        w1_planes = keep.tile([P, HID], U8, align_bytes=256)
        w2_words = keep.tile([P, C_GROUPS, D_OUT], I32, align_bytes=256)
        w2_planes = keep.tile([P, W2_SLOTS, D_OUT], U8, align_bytes=256)
        warm = keep.tile([P, 1], F32)
        zeros = keep.tile([P, N_PASS], BF16)
        bias_rows = keep.tile([P, N_PASS], BF16)
        b1_cols = keep.tile([P, PACK, H_GROUPS], F32)
        b2_all = keep.tile([P, D_OUT], BF16)
        c_codes = keep.tile([P, C_GROUPS, BATCH], I32, align_bytes=256)
        c_planes = keep.tile([P, C_GROUPS, BATCH], U8, align_bytes=256)
        ident_f32 = keep.tile([P, P], F32)
        ident_bf16 = keep.tile([P, P], BF16)

        early_cols = slice(0, 2 * N_PASS)
        late_cols = slice(2 * N_PASS, HID)
        nc.vector.memset(w1_raw_planes[:, early_cols].bitcast(I32), 0)
        nc.vector.memset(zeros[:], 0.0)
        nc.vector.memset(warm[:], 0.0)
        nc.vector.memset(bias_rows[:], 0.0)
        nc.vector.memset(w1_raw_planes[:, late_cols].bitcast(I32), 0)
        nc.vector.memset(w2_planes[:].bitcast(I32), 0)
        make_identity(nc, ident_f32[:])
        make_identity(nc, ident_bf16[:])

        nc.scalar.activation(out=warm[:], in_=warm[:], func=RELU)
        nc.scalar.dma_start(out=bias_rows[0:H_GROUPS, :], in_=b1.rearrange("(j n) -> j n", n=N_PASS))

        x_by_tile = x.rearrange("(r p) d -> p r d", p=P)

        def load_x(first, count):
            tiles = slice(first, first + count)
            nc.sync.dma_start(out=x_sb[:, tiles, :], in_=x_by_tile[:, tiles, :])

        w1_by_partition = W1_words.rearrange("g p n t -> p g (n t)")
        raw_words = []

        def load_w1_piece(j):
            raw = w_stage.tile([P, X_GROUPS, N_PASS], I32, tag="raw", align_bytes=256)
            nc.sync.dma_start(
                out=raw[:],
                in_=w1_by_partition[:, :, piece(j, N_PASS * PACK)].bitcast(I32),
            )
            raw_words.append(raw)

        def load_w1_scales(cols):
            for quad in range(QUADRANTS):
                first = 32 * quad
                nc.sync.dma_start(
                    out=w1_raw_planes[first : first + SCALE_ROWS * X_GROUPS, cols].bitcast(I32),
                    in_=W1_scales[:, piece(quad, SCALE_ROWS), cols].bitcast(I32),
                )

        load_x(0, 2)
        load_w1_scales(early_cols)
        load_w1_piece(0)
        load_x(2, 1)
        load_x(3, 1)
        load_w1_piece(1)
        load_w1_scales(late_cols)
        for j in range(2, H_GROUPS):
            load_w1_piece(j)
        for slot in range(W2_SLOTS):
            groups = min(PLANES, C_GROUPS - slot * PLANES)
            for quad in range(QUADRANTS):
                first = 32 * quad
                nc.sync.dma_start(
                    out=w2_planes[first : first + SCALE_ROWS * groups, slot, :].bitcast(I32),
                    in_=W2_scales[
                        slot * PLANES : slot * PLANES + groups, piece(quad, SCALE_ROWS), :
                    ].bitcast(I32),
                )
        for g in range(C_GROUPS):
            nc.sync.dma_start(
                out=w2_words[:, g, :],
                in_=W2_words[g].rearrange("p n t -> p (n t)").bitcast(I32),
            )
        nc.sync.dma_start(out=b2_all[:], in_=b2.partition_broadcast(P))

        def sort_w1_scales(j):
            nc.vector.tensor_copy(
                out=w1_planes[:, piece(j, N_PASS)].rearrange("p (t m) -> p m t", t=PACK),
                in_=w1_raw_planes[:, piece(j, N_PASS)].rearrange("p (m t) -> p m t", t=PACK),
            )

        def sort_w1_words(j):
            nc.vector.tensor_copy(
                out=w1_words[:, :, piece(j, N_PASS)].rearrange("p g (t m) -> p g m t", t=PACK),
                in_=raw_words[j][:].rearrange("p g (m t) -> p g m t", t=PACK),
            )

        x_pairs = x_sb[:].bitcast(F32)
        pairs_per_pass = K_PASS // 2
        idle_bank = psum.tile([P, N_PASS], F32, tag="bank")

        def keep_warm(count):
            for i in range(count):
                nc.tensor.matmul(out=idle_bank[:], lhsT=zeros[:, 0:P], rhs=zeros[:], start=True, stop=True)

        def turn_x(r):
            x_grouped = x_stage.tile([P, X_GROUPS, P * PACK], BF16, tag="x_grouped", align_bytes=256)
            for g in range(X_GROUPS):
                x_turned = psum.tile([P, 2, P], F32, tag="bank")
                for u in range(2):
                    nc.tensor.transpose(
                        x_turned[:, u, :],
                        x_pairs[:, r, g * pairs_per_pass + u : (g + 1) * pairs_per_pass : 2],
                        ident_f32[:],
                    )
                grouped = x_grouped[:, g, :].bitcast(F32).rearrange("p (b u) -> p b u", u=2)
                turned = x_turned[:].rearrange("p u b -> p b u")
                if g == 0:
                    nc.scalar.copy(out=grouped, in_=turned)
                else:
                    nc.vector.tensor_copy(out=grouped, in_=turned)
            return x_grouped

        def quantise_x(r, x_grouped):
            for g in range(X_GROUPS):
                nc.vector.quantize_mx(
                    out=c_codes[:, g, piece(r, P)].bitcast(FP8X4),
                    scales=c_planes[:, g, piece(r, P)],
                    in_=x_grouped[:, g, :],
                )

        def turn_b1():
            b1_turned = psum.tile([P, PACK, H_GROUPS], F32, tag="bank")
            for t in range(PACK):
                nc.tensor.matmul(
                    out=b1_turned[:, t, :],
                    lhsT=bias_rows[:, t : N_PASS : PACK],
                    rhs=ident_bf16[:, 0:H_GROUPS],
                    start=True,
                    stop=True,
                )
            nc.scalar.copy(out=b1_cols[:], in_=b1_turned[:])

        def open_piece():
            h = h_stage.tile([P, PACK, BATCH], BF16, tag="h")
            banks = []
            for t in range(PACK):
                sums = psum.tile([P, BATCH], F32, tag="bank")
                banks.append(sums)
            return h, banks

        def multiply(j, banks, t, rows):
            cols = piece(j * PACK + t, P)
            for g in range(X_GROUPS):
                nc.tensor.matmul_mx(
                    out=banks[t][:, rows],
                    lhsT=w1_words[:, g, cols].bitcast(FP8X4),
                    lhsT_scale=w1_planes[SCALE_ROWS * g : P, cols],
                    rhs=c_codes[:, g, rows].bitcast(FP8X4),
                    rhs_scale=c_planes[:, g, rows],
                    start=(g == 0),
                    stop=(g == X_GROUPS - 1),
                )
        def add_and_relu(j, h, banks, t, rows):
            nc.scalar.activation(
                out=h[:, t, rows], in_=banks[t][:, rows], func=RELU, bias=b1_cols[:, t, j : j + 1]
            )

        def interleave(h):
            grouped = q_stage.tile([P, BATCH, PACK], BF16, tag="grouped", align_bytes=256)
            nc.vector.tensor_copy(
                out=grouped[:].rearrange("p (c i) t -> p c t i", i=4),
                in_=h[:].rearrange("p t (c i) -> p c t i", i=4),
            )
            return grouped

        def quantise_h(j, grouped):
            nc.vector.quantize_mx(
                out=c_codes[:, X_GROUPS + j, :].bitcast(FP8X4),
                scales=c_planes[:, X_GROUPS + j, :],
                in_=grouped[:].rearrange("p b t -> p (b t)"),
            )

        def second_product_pass(acc, r, first_col, width, g):
            cols = slice(first_col, first_col + width)
            nc.tensor.matmul_mx(
                out=acc[:],
                lhsT=c_codes[:, g, piece(r, P)].bitcast(FP8X4),
                lhsT_scale=c_planes[:, g, piece(r, P)],
                rhs=w2_words[:, g, cols].bitcast(FP8X4),
                rhs_scale=w2_planes[SCALE_ROWS * (g % PLANES) : P, g // PLANES, cols],
                start=(g == 0),
                stop=(g == C_GROUPS - 1),
            )

        def finish(acc, r, first_col, width):
            cols = slice(first_col, first_col + width)
            result = o_stage.tile([P, width], F32, tag="result%d" % width)
            nc.vector.tensor_tensor(out=result[:], in0=acc[:], in1=b2_all[:, cols], op=ADD)
            nc.sync.dma_start(out=out[piece(r, P), cols], in_=result[:])

        def first_piece():
            early, late = piece(0, BATCH // 2), piece(1, BATCH // 2)
            keep_warm(4)
            sort_w1_scales(0)
            sort_w1_scales(1)
            x0 = turn_x(0)
            x1 = turn_x(1)
            quantise_x(0, x0)
            quantise_x(1, x1)
            sort_w1_words(0)
            keep_warm(2)
            x2 = turn_x(2)
            x3 = turn_x(3)
            turn_b1()
            quantise_x(2, x2)
            quantise_x(3, x3)
            h, banks = open_piece()
            for t in range(PACK):
                multiply(0, banks, t, early)
                add_and_relu(0, h, banks, t, early)
            for t in range(PACK):
                multiply(0, banks, t, late)
                add_and_relu(0, h, banks, t, late)
            return h

        h_pieces = []
        grouped = []
        for j in range(H_GROUPS):
            if j == 0:
                h_pieces.append(first_piece())
                sort_w1_words(1)
            else:
                h, banks = open_piece()
                for t in range(PACK):
                    multiply(j, banks, t, slice(0, BATCH))
                    add_and_relu(j, h, banks, t, slice(0, BATCH))
                h_pieces.append(h)
            for ahead in range(2 * j + 2, min(2 * j + 4, H_GROUPS)):
                sort_w1_scales(ahead)
                sort_w1_words(ahead)
            if 2 * j + 2 >= H_GROUPS:
                for done in range(len(grouped), min(len(grouped) + 2, j)):
                    grouped.append(interleave(h_pieces[done]))
                    if done >= 1:
                        quantise_h(done - 1, grouped[done - 1])

        left = []
        for r in range(ROW_TILES):
            acc = psum.tile([P, N_PASS], F32, tag="bank")
            left.append(acc)
        right = []
        for r in range(ROW_TILES - 1):
            acc = psum.tile([P, N_PASS], F32, tag="bank")
            right.append(acc)
        for g in range(X_GROUPS):
            for r in range(ROW_TILES):
                second_product_pass(left[r], r, 0, N_PASS, g)
        for r in range(ROW_TILES - 1):
            for g in range(X_GROUPS):
                second_product_pass(right[r], r, N_PASS, N_PASS, g)
        for done in range(len(grouped), H_GROUPS):
            grouped.append(interleave(h_pieces[done]))
            quantise_h(done - 1, grouped[done - 1])
        quantise_h(H_GROUPS - 1, grouped[H_GROUPS - 1])
        for g in range(X_GROUPS, C_GROUPS):
            for r in range(ROW_TILES):
                second_product_pass(left[r], r, 0, N_PASS, g)
        for r in range(ROW_TILES):
            finish(left[r], r, 0, N_PASS)
        for r in range(ROW_TILES - 1):
            for g in range(X_GROUPS, C_GROUPS):
                second_product_pass(right[r], r, N_PASS, N_PASS, g)
            finish(right[r], r, N_PASS, N_PASS)
        first_col = N_PASS
        for width in [N_PASS // 2, N_PASS // 4, N_PASS // 4]:
            acc = psum.tile([P, width], F32, tag="bank")
            for g in range(C_GROUPS):
                second_product_pass(acc, ROW_TILES - 1, first_col, width, g)
            finish(acc, ROW_TILES - 1, first_col, width)
            first_col += width
